import numpy as np
import ml_dtypes


def mxq(x, axis, fmt="e4m3"):
    dtype, down = {"e4m3": (ml_dtypes.float8_e4m3fn, 7), "e5m2": (ml_dtypes.float8_e5m2, 14)}[fmt]
    v = np.moveaxis(np.asarray(x, np.float32).astype(ml_dtypes.bfloat16).astype(np.float64), axis, -1)
    blocks = v.reshape(v.shape[:-1] + (-1, 32))
    amax = np.abs(blocks).max(-1, keepdims=True)
    byte = np.maximum(np.where(amax > 0, np.frexp(amax)[1] - 1 + 127, 0) - down, 1)
    scale = np.exp2(byte - 127.0)
    codes = (blocks / scale).astype(np.float32).astype(dtype).astype(np.float64)
    return np.moveaxis((codes * scale).reshape(v.shape), -1, axis)


WIDE = False


def mx_kscale(k):
    if not WIDE:
        return np.ones(k)
    levels = np.array([10, -10, 5, -5, 0])
    a = np.random.permutation(np.resize(levels, k // 512 * 4)).reshape(k // 512, 4)
    idx = np.arange(k)
    return np.exp2(a[idx // 512, idx % 128 // 32])


BF16 = ml_dtypes.bfloat16


def bf(x):
    return np.asarray(x, np.float32).astype(BF16)


def f64(x):
    return np.asarray(x).astype(np.float64)


T, D = 1024, 1024


def setup_inputs():
    s = mx_kscale(D)
    w = 1.0 / np.sqrt(D)
    return {"src": bf(np.random.standard_normal((T, D)) * s),
            "theta_k": bf(np.random.standard_normal((D, D)) * w / s[:, None]),
            "theta_v": bf(np.random.standard_normal((D, D)) * w / s[:, None]),
            "W": bf(np.random.standard_normal((D, D)) * w),
            "b": bf(np.random.standard_normal(D) * 0.5)}


def reference(src, theta_k, theta_v, W, b):
    xq = mxq(f64(src), 1, "e4m3")
    train_view = xq @ mxq(f64(theta_k), 0, "e4m3")
    label_view = xq @ mxq(f64(theta_v), 0, "e4m3")
    target = label_view - train_view
    pred = (mxq(train_view, 1, "e4m3") @ mxq(f64(W), 1, "e4m3").T) + f64(b)
    err = pred - target
    return train_view, err

@@ -1,0 +1,227 @@
+from contextlib import ExitStack
+
+import concourse.mybir as mybir
+from concourse.masks import make_identity
+
+F32 = mybir.dt.float32
+BF16 = mybir.dt.bfloat16
+U32 = mybir.dt.uint32
+U8 = mybir.dt.uint8
+FP8X4 = mybir.dt.float8_e4m3fn_x4
+ADD = mybir.AluOpType.add
+
+P = 128
+PACK = 4
+K_PASS = P * PACK
+T = 1024
+D = 1024
+PASSES = D // K_PASS
+BLOCKS = T // P
+N_TILE = 512
+HALVES = D // N_TILE
+
+FLOPS = 3 * 2 * T * D * D
+
+
+def flip_rows_and_quantise(nc, psum, stage, identity, rows, codes, scales):
+    words = rows.bitcast(F32)
+    flipped = psum.tile([P, PASSES, 2, P], F32, tag="flipped")
+    for g in range(PASSES):
+        for u in range(2):
+            first = (2 * g + u) * P
+            nc.tensor.transpose(
+                out=flipped[:, g, u, :], in_=words[:, first : first + P], identity=identity
+            )
+    grouped = stage.tile([P, PASSES * P * PACK], BF16, align_bytes=64, tag="rows_grouped")
+    nc.scalar.copy(
+        out=grouped[:].bitcast(F32).rearrange("p (g r u) -> p g r u", g=PASSES, u=2),
+        in_=flipped[:].rearrange("p g u r -> p g r u"),
+    )
+    for g in range(PASSES):
+        nc.vector.quantize_mx(
+            out=codes[:, g, :].bitcast(FP8X4),
+            scales=scales[:, g, :],
+            in_=grouped[:, g * P * PACK : (g + 1) * P * PACK],
+        )
+
+
+def mx_group(nc, out, products):
+    last = len(products) - 1
+    for n, (stationary, moving) in enumerate(products):
+        nc.tensor.matmul_mx(
+            out=out,
+            lhsT=stationary[0].bitcast(FP8X4),
+            lhsT_scale=stationary[1],
+            rhs=moving[0].bitcast(FP8X4),
+            rhs_scale=moving[1],
+            start=(n == 0),
+            stop=(n == last),
+        )
+
+
+def tile_tttinner_pa_kernel(tc, src, theta_k, theta_v, W, b, out_0, out_1):
+    nc = tc.nc
+    with ExitStack() as ctx:
+        const = ctx.enter_context(tc.tile_pool(name="const", bufs=1))
+        keep = ctx.enter_context(tc.tile_pool(name="keep", bufs=1))
+        stage = ctx.enter_context(tc.tile_pool(name="stage", bufs=3))
+        results = ctx.enter_context(tc.tile_pool(name="results", bufs=4))
+        psum = ctx.enter_context(tc.psum_pool(name="psum", bufs=2))
+
+        src_blocks = src.rearrange("(p j) d -> p j d", j=BLOCKS)
+        train_view_blocks = out_0.rearrange("(p j) d -> p j d", j=BLOCKS)
+        err_blocks = out_1.rearrange("(p j) d -> p j d", j=BLOCKS)
+
+        src_sb = keep.tile([P, BLOCKS, D], BF16)
+        w_sb = keep.tile([P, BLOCKS, D], BF16)
+        theta_k_sb = keep.tile([P, PASSES, PACK, D], BF16)
+        theta_v_sb = keep.tile([P, PASSES, PACK, D], BF16)
+
+        def load_theta(theta, theta_sb, columns):
+            for g in range(PASSES):
+                for u in range(2):
+                    first = g * K_PASS + u * 2 * P
+                    nc.sync.dma_start(
+                        out=theta_sb[:, g, 2 * u : 2 * u + 2, columns],
+                        in_=theta[first : first + 2 * P, columns].rearrange(
+                            "(q e) c -> q e c", e=2
+                        ),
+                    )
+
+        def half(h):
+            return slice(h * N_TILE, (h + 1) * N_TILE)
+
+        def block(i):
+            return slice(i * P, (i + 1) * P)
+
+        load_theta(theta_k, theta_k_sb, half(0))
+        for j in range(0, BLOCKS, 2):
+            nc.sync.dma_start(out=src_sb[:, j : j + 2, :], in_=src_blocks[:, j : j + 2, :])
+        load_theta(theta_k, theta_k_sb, half(1))
+        load_theta(theta_v, theta_v_sb, slice(0, D))
+        for j in range(0, BLOCKS, 2):
+            nc.sync.dma_start(
+                out=w_sb[:, j : j + 2, :],
+                in_=W[j * P : (j + 2) * P, :].rearrange("(j p) f -> p j f", p=P),
+            )
+
+        identity = const.tile([P, P], F32)
+        make_identity(nc, identity[:])
+        ones = const.tile([P, P], BF16)
+        nc.vector.memset(ones[:], 1.0)
+        bias_row = const.tile([P, D], BF16)
+        nc.vector.memset(bias_row[:], 0.0)
+        nc.scalar.dma_start(out=bias_row[0:1, :], in_=b.rearrange("(o n) -> o n", o=1))
+        bias_sb = const.tile([P, D], F32)
+        for h in range(HALVES):
+            bias_ps = psum.tile([P, N_TILE], F32, tag="flipped")
+            nc.tensor.matmul(
+                out=bias_ps[:], lhsT=ones[:], rhs=bias_row[:, half(h)], start=True, stop=True
+            )
+            nc.scalar.copy(out=bias_sb[:, half(h)], in_=bias_ps[:])
+
+        def operand(name):
+            words = keep.tile([P, PASSES, D], U32, align_bytes=64, name=name + "_words")
+            scales = keep.tile([P, PASSES, D], U8, align_bytes=64, name=name + "_scales")
+            return words, scales
+
+        src_q = operand("src")
+        theta_k_q = operand("theta_k")
+        minus_theta_v_q = operand("minus_theta_v")
+        w_q = operand("w")
+        train_view_q = operand("train_view")
+
+        def view(op, g, columns):
+            return op[0][:, g, columns], op[1][:, g, columns]
+
+        def quantise_theta_k(g, h):
+            grouped = stage.tile([P, N_TILE * PACK], BF16, align_bytes=64, tag="theta_grouped")
+            sorted_out = grouped[:].rearrange("p (a e q t) -> p e a q t", a=2, e=2, t=PACK)
+            sorted_in = theta_k_sb[:, g, :, half(h)].rearrange(
+                "p t (a q e) -> p e a q t", a=2, e=2
+            )
+            for e in range(2):
+                nc.vector.tensor_copy(out=sorted_out[:, e], in_=sorted_in[:, e])
+            words, scales = view(theta_k_q, g, half(h))
+            nc.vector.quantize_mx(out=words.bitcast(FP8X4), scales=scales, in_=grouped[:])
+
+        def quantise_minus_theta_v(g, h):
+            grouped = stage.tile([P, N_TILE * PACK], BF16, align_bytes=64, tag="theta_grouped")
+            nc.vector.tensor_scalar_mul(
+                out=grouped[:].rearrange("p (c i t) -> p c t i", i=4, t=PACK),
+                in0=theta_v_sb[:, g, :, half(h)].rearrange("p t (c i) -> p c t i", i=4),
+                scalar1=-1.0,
+            )
+            words, scales = view(minus_theta_v_q, g, half(h))
+            nc.vector.quantize_mx(out=words.bitcast(FP8X4), scales=scales, in_=grouped[:])
+
+        def quantise_rows(rows_sb, op, i):
+            flip_rows_and_quantise(
+                nc, psum, stage, identity[:], rows_sb[:, i, :],
+                op[0][:, :, block(i)], op[1][:, :, block(i)],
+            )
+
+        for g in range(PASSES):
+            quantise_theta_k(g, 0)
+        for i in range(BLOCKS):
+            quantise_rows(src_sb, src_q, i)
+        for g in range(PASSES):
+            quantise_theta_k(g, 1)
+
+        train_view_sb = keep.tile([P, BLOCKS, D], F32)
+        for h in range(HALVES):
+            for i in range(BLOCKS):
+                tv_ps = psum.tile([P, N_TILE], F32, tag="tv")
+                mx_group(
+                    nc, tv_ps[:],
+                    [(view(src_q, c, block(i)), view(theta_k_q, c, half(h))) for c in range(PASSES)],
+                )
+                nc.scalar.copy(
+                    out=train_view_sb[:, i, half(h)].rearrange("p (a q e) -> p a q e", a=2, e=2),
+                    in_=tv_ps[:].rearrange("p (a e q) -> p a q e", a=2, e=2),
+                )
+                nc.sync.dma_start(
+                    out=train_view_blocks[:, i, half(h)], in_=train_view_sb[:, i, half(h)]
+                )
+
+                tv_flipped = psum.tile([P, PACK, P], F32, tag="tv_flipped")
+                for t in range(PACK):
+                    mx_group(
+                        nc, tv_flipped[:, t, :],
+                        [
+                            (view(theta_k_q, c, block(PACK * h + t)), view(src_q, c, block(i)))
+                            for c in range(PASSES)
+                        ],
+                    )
+                tv_grouped = stage.tile([P, P * PACK], BF16, align_bytes=64, tag="tv_grouped")
+                nc.scalar.copy(
+                    out=tv_grouped[:].rearrange("p (r t) -> p r t", t=PACK),
+                    in_=tv_flipped[:].rearrange("p t r -> p r t"),
+                )
+                words, scales = view(train_view_q, h, block(i))
+                nc.vector.quantize_mx(out=words.bitcast(FP8X4), scales=scales, in_=tv_grouped[:])
+
+            if h == 0:
+                for g in range(PASSES):
+                    for hv in range(HALVES):
+                        quantise_minus_theta_v(g, hv)
+
+        for i in range(BLOCKS):
+            quantise_rows(w_sb, w_q, i)
+
+        for i in range(BLOCKS):
+            nc.vector.tensor_tensor(
+                out=train_view_sb[:, i, :], in0=train_view_sb[:, i, :], in1=bias_sb[:], op=ADD
+            )
+            for h in range(HALVES):
+                err_ps = psum.tile([P, N_TILE], F32, tag="err")
+                mx_group(
+                    nc, err_ps[:],
+                    [(view(src_q, c, block(i)), view(minus_theta_v_q, c, half(h))) for c in range(PASSES)]
+                    + [(view(train_view_q, g, block(i)), view(w_q, g, half(h))) for g in range(PASSES)],
+                )
+                err_sb = results.tile([P, N_TILE], F32)
+                nc.vector.tensor_tensor(
+                    out=err_sb[:], in0=err_ps[:], in1=train_view_sb[:, i, half(h)], op=ADD
+                )
+                nc.sync.dma_start(out=err_blocks[:, i, half(h)], in_=err_sb[:])

@@ -64,9 +64,11 @@ def tile_tttinner_pa_kernel(tc, src, theta_k, theta_v, W, b, out_0, out_1):
     with ExitStack() as ctx:
         const = ctx.enter_context(tc.tile_pool(name="const", bufs=1))
         keep = ctx.enter_context(tc.tile_pool(name="keep", bufs=1))
-        stage = ctx.enter_context(tc.tile_pool(name="stage", bufs=3))
+        stage = ctx.enter_context(tc.tile_pool(name="stage", bufs=4))
         results = ctx.enter_context(tc.tile_pool(name="results", bufs=4))
         psum = ctx.enter_context(tc.psum_pool(name="psum", bufs=2))
+        sums = ctx.enter_context(tc.psum_pool(name="sums", bufs=6))
+        ctx.enter_context(tc.manual_schedule())
 
         src_blocks = src.rearrange("(p j) d -> p j d", j=BLOCKS)
         train_view_blocks = out_0.rearrange("(p j) d -> p j d", j=BLOCKS)
@@ -94,6 +96,9 @@ def tile_tttinner_pa_kernel(tc, src, theta_k, theta_v, W, b, out_0, out_1):
         def block(i):
             return slice(i * P, (i + 1) * P)
 
+        bias_row = const.tile([P, D], BF16)
+        nc.vector.memset(bias_row[:], 0.0)
+        nc.sync.dma_start(out=bias_row[0:1, :], in_=b.rearrange("(o n) -> o n", o=1))
         load_theta(theta_k, theta_k_sb, half(0))
         for j in range(0, BLOCKS, 2):
             nc.sync.dma_start(out=src_sb[:, j : j + 2, :], in_=src_blocks[:, j : j + 2, :])
@@ -109,12 +114,9 @@ def tile_tttinner_pa_kernel(tc, src, theta_k, theta_v, W, b, out_0, out_1):
         make_identity(nc, identity[:])
         ones = const.tile([P, P], BF16)
         nc.vector.memset(ones[:], 1.0)
-        bias_row = const.tile([P, D], BF16)
-        nc.vector.memset(bias_row[:], 0.0)
-        nc.scalar.dma_start(out=bias_row[0:1, :], in_=b.rearrange("(o n) -> o n", o=1))
         bias_sb = const.tile([P, D], F32)
         for h in range(HALVES):
-            bias_ps = psum.tile([P, N_TILE], F32, tag="flipped")
+            bias_ps = sums.tile([P, N_TILE], F32, tag="sum")
             nc.tensor.matmul(
                 out=bias_ps[:], lhsT=ones[:], rhs=bias_row[:, half(h)], start=True, stop=True
             )
@@ -134,7 +136,7 @@ def tile_tttinner_pa_kernel(tc, src, theta_k, theta_v, W, b, out_0, out_1):
         def view(op, g, columns):
             return op[0][:, g, columns], op[1][:, g, columns]
 
-        def quantise_theta_k(g, h):
+        def regroup_theta_k(g, h):
             grouped = stage.tile([P, N_TILE * PACK], BF16, align_bytes=64, tag="theta_grouped")
             sorted_out = grouped[:].rearrange("p (a e q t) -> p e a q t", a=2, e=2, t=PACK)
             sorted_in = theta_k_sb[:, g, :, half(h)].rearrange(
@@ -142,17 +144,19 @@ def tile_tttinner_pa_kernel(tc, src, theta_k, theta_v, W, b, out_0, out_1):
             )
             for e in range(2):
                 nc.vector.tensor_copy(out=sorted_out[:, e], in_=sorted_in[:, e])
-            words, scales = view(theta_k_q, g, half(h))
-            nc.vector.quantize_mx(out=words.bitcast(FP8X4), scales=scales, in_=grouped[:])
+            return grouped
 
-        def quantise_minus_theta_v(g, h):
+        def regroup_minus_theta_v(g, h):
             grouped = stage.tile([P, N_TILE * PACK], BF16, align_bytes=64, tag="theta_grouped")
             nc.vector.tensor_scalar_mul(
                 out=grouped[:].rearrange("p (c i t) -> p c t i", i=4, t=PACK),
                 in0=theta_v_sb[:, g, :, half(h)].rearrange("p t (c i) -> p c t i", i=4),
                 scalar1=-1.0,
             )
-            words, scales = view(minus_theta_v_q, g, half(h))
+            return grouped
+
+        def quantise_theta(grouped, op, g, h):
+            words, scales = view(op, g, half(h))
             nc.vector.quantize_mx(out=words.bitcast(FP8X4), scales=scales, in_=grouped[:])
 
         def quantise_rows(rows_sb, op, i):
@@ -161,17 +165,41 @@ def tile_tttinner_pa_kernel(tc, src, theta_k, theta_v, W, b, out_0, out_1):
                 op[0][:, :, block(i)], op[1][:, :, block(i)],
             )
 
+        first_grouped = [regroup_theta_k(g, 0) for g in range(PASSES)]
         for g in range(PASSES):
-            quantise_theta_k(g, 0)
-        for i in range(BLOCKS):
+            quantise_theta(first_grouped[g], theta_k_q, g, 0)
+        for i in range(2):
             quantise_rows(src_sb, src_q, i)
-        for g in range(PASSES):
-            quantise_theta_k(g, 1)
+
+        later_pieces = [(regroup_theta_k, theta_k_q, g, 1) for g in range(PASSES)] + [
+            (regroup_minus_theta_v, minus_theta_v_q, g, h)
+            for g in range(PASSES)
+            for h in range(HALVES)
+        ]
+
+        def add_bias(i, h):
+            nc.vector.tensor_tensor(
+                out=train_view_sb[:, i, half(h)],
+                in0=train_view_sb[:, i, half(h)],
+                in1=bias_sb[:, half(h)],
+                op=ADD,
+            )
+
+        def quantise_train_view(tv_grouped, h, i):
+            words, scales = view(train_view_q, h, block(i))
+            nc.vector.quantize_mx(out=words.bitcast(FP8X4), scales=scales, in_=tv_grouped[:])
 
         train_view_sb = keep.tile([P, BLOCKS, D], F32)
         for h in range(HALVES):
             for i in range(BLOCKS):
-                tv_ps = psum.tile([P, N_TILE], F32, tag="tv")
+                if i % 2 == 0 and h == 0 and i + 2 < BLOCKS:
+                    quantise_rows(src_sb, src_q, i + 2)
+                    quantise_rows(src_sb, src_q, i + 3)
+                if i % 2 == 0 and h == 1:
+                    quantise_rows(w_sb, w_q, i)
+                    quantise_rows(w_sb, w_q, i + 1)
+
+                tv_ps = sums.tile([P, N_TILE], F32, tag="sum")
                 mx_group(
                     nc, tv_ps[:],
                     [(view(src_q, c, block(i)), view(theta_k_q, c, half(h))) for c in range(PASSES)],
@@ -184,7 +212,7 @@ def tile_tttinner_pa_kernel(tc, src, theta_k, theta_v, W, b, out_0, out_1):
                     out=train_view_blocks[:, i, half(h)], in_=train_view_sb[:, i, half(h)]
                 )
 
-                tv_flipped = psum.tile([P, PACK, P], F32, tag="tv_flipped")
+                tv_flipped = sums.tile([P, PACK, P], F32, tag="sum")
                 for t in range(PACK):
                     mx_group(
                         nc, tv_flipped[:, t, :],
@@ -193,28 +221,28 @@ def tile_tttinner_pa_kernel(tc, src, theta_k, theta_v, W, b, out_0, out_1):
                             for c in range(PASSES)
                         ],
                     )
+                step = h * BLOCKS + i
+                if step // 2 < len(later_pieces):
+                    regroup, op, g, hp = later_pieces[step // 2]
+                    if step % 2 == 0:
+                        piece_grouped = regroup(g, hp)
+                    else:
+                        quantise_theta(piece_grouped, op, g, hp)
+                if i > 0:
+                    quantise_train_view(tv_grouped, h, i - 1)
                 tv_grouped = stage.tile([P, P * PACK], BF16, align_bytes=64, tag="tv_grouped")
                 nc.scalar.copy(
                     out=tv_grouped[:].rearrange("p (r t) -> p r t", t=PACK),
                     in_=tv_flipped[:].rearrange("p t r -> p r t"),
                 )
-                words, scales = view(train_view_q, h, block(i))
-                nc.vector.quantize_mx(out=words.bitcast(FP8X4), scales=scales, in_=tv_grouped[:])
+                if h == 1:
+                    add_bias(i, 0)
+            quantise_train_view(tv_grouped, h, BLOCKS - 1)
 
-            if h == 0:
-                for g in range(PASSES):
-                    for hv in range(HALVES):
-                        quantise_minus_theta_v(g, hv)
-
+        add_bias(0, 1)
         for i in range(BLOCKS):
-            quantise_rows(w_sb, w_q, i)
-
-        for i in range(BLOCKS):
-            nc.vector.tensor_tensor(
-                out=train_view_sb[:, i, :], in0=train_view_sb[:, i, :], in1=bias_sb[:], op=ADD
-            )
             for h in range(HALVES):
-                err_ps = psum.tile([P, N_TILE], F32, tag="err")
+                err_ps = sums.tile([P, N_TILE], F32, tag="sum")
                 mx_group(
                     nc, err_ps[:],
                     [(view(src_q, c, block(i)), view(minus_theta_v_q, c, half(h))) for c in range(PASSES)]
@@ -225,3 +253,5 @@ def tile_tttinner_pa_kernel(tc, src, theta_k, theta_v, W, b, out_0, out_1):
                     out=err_sb[:], in0=err_ps[:], in1=train_view_sb[:, i, half(h)], op=ADD
                 )
                 nc.sync.dma_start(out=err_blocks[:, i, half(h)], in_=err_sb[:])
+                if h == 0 and i + 1 < BLOCKS:
+                    add_bias(i + 1, 1)

@@ -76,15 +76,15 @@ def tile_tttinner_pa_kernel(tc, src, theta_k, theta_v, W, b, out_0, out_1):
 
         src_sb = keep.tile([P, BLOCKS, D], BF16)
         w_sb = keep.tile([P, BLOCKS, D], BF16)
-        theta_k_sb = keep.tile([P, PASSES, PACK, D], BF16)
+        theta_k_sb = keep.tile([P, HALVES, PASSES, PACK, N_TILE], BF16)
         theta_v_sb = keep.tile([P, PASSES, PACK, D], BF16)
 
-        def load_theta(theta, theta_sb, columns):
+        def load_theta(theta, columns, rows_of_pass):
             for g in range(PASSES):
                 for u in range(2):
                     first = g * K_PASS + u * 2 * P
                     nc.sync.dma_start(
-                        out=theta_sb[:, g, 2 * u : 2 * u + 2, columns],
+                        out=rows_of_pass(g)[:, 2 * u : 2 * u + 2, :],
                         in_=theta[first : first + 2 * P, columns].rearrange(
                             "(q e) c -> q e c", e=2
                         ),
@@ -98,12 +98,14 @@ def tile_tttinner_pa_kernel(tc, src, theta_k, theta_v, W, b, out_0, out_1):
 
         bias_row = const.tile([P, D], BF16)
         nc.vector.memset(bias_row[:], 0.0)
-        nc.sync.dma_start(out=bias_row[0:1, :], in_=b.rearrange("(o n) -> o n", o=1))
-        load_theta(theta_k, theta_k_sb, half(0))
+        ones = const.tile([P, P], BF16)
+        nc.vector.memset(ones[:], 1.0)
+        nc.scalar.dma_start(out=bias_row[0:1, :], in_=b.rearrange("(o n) -> o n", o=1))
+        load_theta(theta_k, half(0), lambda g: theta_k_sb[:, 0, g])
         for j in range(0, BLOCKS, 2):
             nc.sync.dma_start(out=src_sb[:, j : j + 2, :], in_=src_blocks[:, j : j + 2, :])
-        load_theta(theta_k, theta_k_sb, half(1))
-        load_theta(theta_v, theta_v_sb, slice(0, D))
+        load_theta(theta_k, half(1), lambda g: theta_k_sb[:, 1, g])
+        load_theta(theta_v, slice(0, D), lambda g: theta_v_sb[:, g])
         for j in range(0, BLOCKS, 2):
             nc.sync.dma_start(
                 out=w_sb[:, j : j + 2, :],
@@ -112,16 +114,6 @@ def tile_tttinner_pa_kernel(tc, src, theta_k, theta_v, W, b, out_0, out_1):
 
         identity = const.tile([P, P], F32)
         make_identity(nc, identity[:])
-        ones = const.tile([P, P], BF16)
-        nc.vector.memset(ones[:], 1.0)
-        bias_sb = const.tile([P, D], F32)
-        for h in range(HALVES):
-            bias_ps = sums.tile([P, N_TILE], F32, tag="sum")
-            nc.tensor.matmul(
-                out=bias_ps[:], lhsT=ones[:], rhs=bias_row[:, half(h)], start=True, stop=True
-            )
-            nc.scalar.copy(out=bias_sb[:, half(h)], in_=bias_ps[:])
-
         def operand(name):
             words = keep.tile([P, PASSES, D], U32, align_bytes=64, name=name + "_words")
             scales = keep.tile([P, PASSES, D], U8, align_bytes=64, name=name + "_scales")
@@ -138,10 +130,8 @@ def tile_tttinner_pa_kernel(tc, src, theta_k, theta_v, W, b, out_0, out_1):
 
         def regroup_theta_k(g, h):
             grouped = stage.tile([P, N_TILE * PACK], BF16, align_bytes=64, tag="theta_grouped")
-            sorted_out = grouped[:].rearrange("p (a e q t) -> p e a q t", a=2, e=2, t=PACK)
-            sorted_in = theta_k_sb[:, g, :, half(h)].rearrange(
-                "p t (a q e) -> p e a q t", a=2, e=2
-            )
+            sorted_out = grouped[:].rearrange("p (e u q t) -> p e u q t", e=2, u=2, t=PACK)
+            sorted_in = theta_k_sb[:, h, g].rearrange("p t (u q e) -> p e u q t", u=2, e=2)
             for e in range(2):
                 nc.vector.tensor_copy(out=sorted_out[:, e], in_=sorted_in[:, e])
             return grouped
@@ -170,6 +160,14 @@ def tile_tttinner_pa_kernel(tc, src, theta_k, theta_v, W, b, out_0, out_1):
             quantise_theta(first_grouped[g], theta_k_q, g, 0)
         for i in range(2):
             quantise_rows(src_sb, src_q, i)
+
+        bias_sb = const.tile([P, D], F32)
+        for h in range(HALVES):
+            bias_ps = sums.tile([P, N_TILE], F32, tag="sum")
+            nc.tensor.matmul(
+                out=bias_ps[:], lhsT=ones[:], rhs=bias_row[:, half(h)], start=True, stop=True
+            )
+            nc.scalar.copy(out=bias_sb[:, half(h)], in_=bias_ps[:])
 
         later_pieces = [(regroup_theta_k, theta_k_q, g, 1) for g in range(PASSES)] + [
             (regroup_minus_theta_v, minus_theta_v_q, g, h)
@@ -205,8 +203,8 @@ def tile_tttinner_pa_kernel(tc, src, theta_k, theta_v, W, b, out_0, out_1):
                     [(view(src_q, c, block(i)), view(theta_k_q, c, half(h))) for c in range(PASSES)],
                 )
                 nc.scalar.copy(
-                    out=train_view_sb[:, i, half(h)].rearrange("p (a q e) -> p a q e", a=2, e=2),
-                    in_=tv_ps[:].rearrange("p (a e q) -> p a q e", a=2, e=2),
+                    out=train_view_sb[:, i, half(h)].rearrange("p (u q e) -> p u q e", u=2, e=2),
+                    in_=tv_ps[:].rearrange("p (e u q) -> p u q e", e=2, u=2),
                 )
                 nc.sync.dma_start(
                     out=train_view_blocks[:, i, half(h)], in_=train_view_sb[:, i, half(h)]
@@ -214,10 +212,11 @@ def tile_tttinner_pa_kernel(tc, src, theta_k, theta_v, W, b, out_0, out_1):
 
                 tv_flipped = sums.tile([P, PACK, P], F32, tag="sum")
                 for t in range(PACK):
+                    u, e = divmod(t, 2)
                     mx_group(
                         nc, tv_flipped[:, t, :],
                         [
-                            (view(theta_k_q, c, block(PACK * h + t)), view(src_q, c, block(i)))
+                            (view(theta_k_q, c, block(PACK * h + 2 * e + u)), view(src_q, c, block(i)))
                             for c in range(PASSES)
                         ],
                     )

@@ -23,28 +23,6 @@ HALVES = D // N_TILE
 FLOPS = 3 * 2 * T * D * D
 
 
-def flip_rows_and_quantise(nc, psum, stage, identity, rows, codes, scales):
-    words = rows.bitcast(F32)
-    flipped = psum.tile([P, PASSES, 2, P], F32, tag="flipped")
-    for g in range(PASSES):
-        for u in range(2):
-            first = (2 * g + u) * P
-            nc.tensor.transpose(
-                out=flipped[:, g, u, :], in_=words[:, first : first + P], identity=identity
-            )
-    grouped = stage.tile([P, PASSES * P * PACK], BF16, align_bytes=64, tag="rows_grouped")
-    nc.scalar.copy(
-        out=grouped[:].bitcast(F32).rearrange("p (g r u) -> p g r u", g=PASSES, u=2),
-        in_=flipped[:].rearrange("p g u r -> p g r u"),
-    )
-    for g in range(PASSES):
-        nc.vector.quantize_mx(
-            out=codes[:, g, :].bitcast(FP8X4),
-            scales=scales[:, g, :],
-            in_=grouped[:, g * P * PACK : (g + 1) * P * PACK],
-        )
-
-
 def mx_group(nc, out, products):
     last = len(products) - 1
     for n, (stationary, moving) in enumerate(products):
@@ -65,7 +43,7 @@ def tile_tttinner_pa_kernel(tc, src, theta_k, theta_v, W, b, out_0, out_1):
         const = ctx.enter_context(tc.tile_pool(name="const", bufs=1))
         keep = ctx.enter_context(tc.tile_pool(name="keep", bufs=1))
         stage = ctx.enter_context(tc.tile_pool(name="stage", bufs=4))
-        results = ctx.enter_context(tc.tile_pool(name="results", bufs=4))
+        results = ctx.enter_context(tc.tile_pool(name="results", bufs=6))
         psum = ctx.enter_context(tc.psum_pool(name="psum", bufs=2))
         sums = ctx.enter_context(tc.psum_pool(name="sums", bufs=6))
         ctx.enter_context(tc.manual_schedule())
@@ -79,61 +57,111 @@ def tile_tttinner_pa_kernel(tc, src, theta_k, theta_v, W, b, out_0, out_1):
         theta_k_sb = keep.tile([P, HALVES, PASSES, PACK, N_TILE], BF16)
         theta_v_sb = keep.tile([P, PASSES, PACK, D], BF16)
 
-        def load_theta(theta, columns, rows_of_pass):
-            for g in range(PASSES):
-                for u in range(2):
-                    first = g * K_PASS + u * 2 * P
-                    nc.sync.dma_start(
-                        out=rows_of_pass(g)[:, 2 * u : 2 * u + 2, :],
-                        in_=theta[first : first + 2 * P, columns].rearrange(
-                            "(q e) c -> q e c", e=2
-                        ),
-                    )
-
         def half(h):
             return slice(h * N_TILE, (h + 1) * N_TILE)
 
         def block(i):
             return slice(i * P, (i + 1) * P)
 
+        def pair(j):
+            return slice(2 * j * P, (2 * j + 2) * P)
+
+        def load_src(j, n):
+            nc.sync.dma_start(out=src_sb[:, j : j + n, :], in_=src_blocks[:, j : j + n, :])
+
+        def load_theta(theta, columns, g, out):
+            for u in range(2):
+                first = g * K_PASS + u * 2 * P
+                nc.sync.dma_start(
+                    out=out[:, 2 * u : 2 * u + 2, :],
+                    in_=theta[first : first + 2 * P, columns].rearrange("(q e) c -> q e c", e=2),
+                )
+
+        identity = const.tile([P, P], F32)
+        make_identity(nc, identity[:])
         bias_row = const.tile([P, D], BF16)
-        nc.vector.memset(bias_row[:], 0.0)
+        nc.gpsimd.memset(bias_row[:], 0.0)
         ones = const.tile([P, P], BF16)
-        nc.vector.memset(ones[:], 1.0)
-        nc.scalar.dma_start(out=bias_row[0:1, :], in_=b.rearrange("(o n) -> o n", o=1))
-        load_theta(theta_k, half(0), lambda g: theta_k_sb[:, 0, g])
-        for j in range(0, BLOCKS, 2):
-            nc.sync.dma_start(out=src_sb[:, j : j + 2, :], in_=src_blocks[:, j : j + 2, :])
-        load_theta(theta_k, half(1), lambda g: theta_k_sb[:, 1, g])
-        load_theta(theta_v, slice(0, D), lambda g: theta_v_sb[:, g])
+        nc.gpsimd.memset(ones[:], 1.0)
+
+        for g in range(PASSES):
+            load_theta(theta_k, half(0), g, theta_k_sb[:, 0, g])
+        load_src(0, 2)
+        nc.sync.dma_start(out=bias_row[0:1, :], in_=b.rearrange("(o n) -> o n", o=1))
+        for j in range(2, BLOCKS, 2):
+            load_src(j, 2)
+        for g in range(PASSES):
+            load_theta(theta_k, half(1), g, theta_k_sb[:, 1, g])
+        for g in range(PASSES):
+            load_theta(theta_v, slice(0, D), g, theta_v_sb[:, g])
         for j in range(0, BLOCKS, 2):
             nc.sync.dma_start(
                 out=w_sb[:, j : j + 2, :],
                 in_=W[j * P : (j + 2) * P, :].rearrange("(j p) f -> p j f", p=P),
             )
 
-        identity = const.tile([P, P], F32)
-        make_identity(nc, identity[:])
-        def operand(name):
-            words = keep.tile([P, PASSES, D], U32, align_bytes=64, name=name + "_words")
-            scales = keep.tile([P, PASSES, D], U8, align_bytes=64, name=name + "_scales")
+
+        def operand(name, shape):
+            words = keep.tile(shape, U32, align_bytes=64, name=name + "_words")
+            scales = keep.tile(shape, U8, align_bytes=64, name=name + "_scales")
             return words, scales
 
-        src_q = operand("src")
-        theta_k_q = operand("theta_k")
-        minus_theta_v_q = operand("minus_theta_v")
-        w_q = operand("w")
-        train_view_q = operand("train_view")
+        src_q = operand("src", [P, BLOCKS, PASSES, P])
+        theta_k_q = operand("theta_k", [P, PASSES, D])
+        minus_theta_v_q = operand("minus_theta_v", [P, PASSES, D])
+        w_q = operand("w", [P, PASSES, D])
+        train_view_q = operand("train_view", [P, PASSES, D])
 
         def view(op, g, columns):
             return op[0][:, g, columns], op[1][:, g, columns]
 
+        def src_rows(i, g):
+            return src_q[0][:, i, g, :], src_q[1][:, i, g, :]
+
+        def quantise(operand_view, grouped):
+            words, scales = operand_view
+            nc.vector.quantize_mx(out=words.bitcast(FP8X4), scales=scales, in_=grouped)
+
+        def turn(rows):
+            words = rows.bitcast(F32)
+            turned = psum.tile([P, PASSES, 2, P], F32, tag="turned")
+            for g in range(PASSES):
+                for u in range(2):
+                    first = (2 * g + u) * P
+                    nc.tensor.transpose(
+                        out=turned[:, g, u, :], in_=words[:, first : first + P], identity=identity[:]
+                    )
+            return turned
+
+        def group_src(turned):
+            grouped = stage.tile([P, PASSES * P * PACK], BF16, align_bytes=64, tag="src_grouped")
+            nc.scalar.copy(
+                out=grouped[:].bitcast(F32).rearrange("p (g r u) -> p g r u", g=PASSES, u=2),
+                in_=turned[:].rearrange("p g u r -> p g r u"),
+            )
+            return grouped
+
+        def quantise_src(grouped, i):
+            words, scales = src_q[0][:, i], src_q[1][:, i]
+            quantise((words.rearrange("p g r -> p (g r)"), scales.rearrange("p g r -> p (g r)")), grouped[:])
+
+        def group_w(turned):
+            grouped = stage.tile([P, PASSES * 2 * P * PACK], BF16, align_bytes=64, tag="w_grouped")
+            words = grouped[:].bitcast(F32).rearrange("p (g n r u) -> p n g r u", g=PASSES, n=2, u=2)
+            for n in range(2):
+                nc.scalar.copy(out=words[:, n], in_=turned[n][:].rearrange("p g u r -> p g r u"))
+            return grouped
+
+        def quantise_w(grouped, j):
+            for g in range(PASSES):
+                quantise(view(w_q, g, pair(j)), grouped[:, 2 * g * K_PASS : 2 * (g + 1) * K_PASS])
+
         def regroup_theta_k(g, h):
             grouped = stage.tile([P, N_TILE * PACK], BF16, align_bytes=64, tag="theta_grouped")
-            sorted_out = grouped[:].rearrange("p (e u q t) -> p e u q t", e=2, u=2, t=PACK)
-            sorted_in = theta_k_sb[:, h, g].rearrange("p t (u q e) -> p e u q t", u=2, e=2)
-            for e in range(2):
-                nc.vector.tensor_copy(out=sorted_out[:, e], in_=sorted_in[:, e])
+            nc.vector.tensor_copy(
+                out=grouped[:].rearrange("p (e c t) -> p e c t", e=2, t=PACK),
+                in_=theta_k_sb[:, h, g].rearrange("p t (c e) -> p e c t", e=2),
+            )
             return grouped
 
         def regroup_minus_theta_v(g, h):
@@ -145,29 +173,37 @@ def tile_tttinner_pa_kernel(tc, src, theta_k, theta_v, W, b, out_0, out_1):
             )
             return grouped
 
-        def quantise_theta(grouped, op, g, h):
-            words, scales = view(op, g, half(h))
-            nc.vector.quantize_mx(out=words.bitcast(FP8X4), scales=scales, in_=grouped[:])
-
-        def quantise_rows(rows_sb, op, i):
-            flip_rows_and_quantise(
-                nc, psum, stage, identity[:], rows_sb[:, i, :],
-                op[0][:, :, block(i)], op[1][:, :, block(i)],
-            )
-
-        first_grouped = [regroup_theta_k(g, 0) for g in range(PASSES)]
-        for g in range(PASSES):
-            quantise_theta(first_grouped[g], theta_k_q, g, 0)
-        for i in range(2):
-            quantise_rows(src_sb, src_q, i)
-
         bias_sb = const.tile([P, D], F32)
-        for h in range(HALVES):
-            bias_ps = sums.tile([P, N_TILE], F32, tag="sum")
-            nc.tensor.matmul(
-                out=bias_ps[:], lhsT=ones[:], rhs=bias_row[:, half(h)], start=True, stop=True
+
+        def spread_bias(copies):
+            for h in range(HALVES):
+                bias_ps = sums.tile([P, N_TILE], F32, tag="sum")
+                nc.tensor.matmul(
+                    out=bias_ps[:], lhsT=ones[:], rhs=bias_row[:, half(h)], start=True, stop=True
+                )
+                copies(out=bias_sb[:, half(h)], in_=bias_ps[:])
+
+        train_view_sb = keep.tile([P, BLOCKS, D], F32)
+        biased = {}
+
+        def add_bias(i, h, engine):
+            if h == 0:
+                with_bias = train_view_sb[:, i, half(0)]
+            else:
+                with_bias = results.tile([P, N_TILE], F32, bufs=4, name="with_bias")[:]
+            engine.tensor_tensor(
+                out=with_bias, in0=train_view_sb[:, i, half(h)], in1=bias_sb[:, half(h)], op=ADD
             )
-            nc.scalar.copy(out=bias_sb[:, half(h)], in_=bias_ps[:])
+            biased[i, h] = with_bias
+
+        theta_grouped = [regroup_theta_k(g, 0) for g in range(PASSES)]
+        for g in range(PASSES):
+            quantise(view(theta_k_q, g, half(0)), theta_grouped[g][:])
+        turned = [turn(src_sb[:, i, :]) for i in range(2)]
+        for i in range(2):
+            quantise_src(group_src(turned[i]), i)
+        spread_bias(nc.vector.tensor_copy)
+
 
         later_pieces = [(regroup_theta_k, theta_k_q, g, 1) for g in range(PASSES)] + [
             (regroup_minus_theta_v, minus_theta_v_q, g, h)
@@ -175,32 +211,20 @@ def tile_tttinner_pa_kernel(tc, src, theta_k, theta_v, W, b, out_0, out_1):
             for h in range(HALVES)
         ]
 
-        def add_bias(i, h):
-            nc.vector.tensor_tensor(
-                out=train_view_sb[:, i, half(h)],
-                in0=train_view_sb[:, i, half(h)],
-                in1=bias_sb[:, half(h)],
-                op=ADD,
-            )
-
-        def quantise_train_view(tv_grouped, h, i):
-            words, scales = view(train_view_q, h, block(i))
-            nc.vector.quantize_mx(out=words.bitcast(FP8X4), scales=scales, in_=tv_grouped[:])
-
-        train_view_sb = keep.tile([P, BLOCKS, D], F32)
         for h in range(HALVES):
             for i in range(BLOCKS):
                 if i % 2 == 0 and h == 0 and i + 2 < BLOCKS:
-                    quantise_rows(src_sb, src_q, i + 2)
-                    quantise_rows(src_sb, src_q, i + 3)
+                    turned = [turn(src_sb[:, i + 2 + n, :]) for n in range(2)]
+                    for n in range(2):
+                        quantise_src(group_src(turned[n]), i + 2 + n)
                 if i % 2 == 0 and h == 1:
-                    quantise_rows(w_sb, w_q, i)
-                    quantise_rows(w_sb, w_q, i + 1)
+                    turned = [turn(w_sb[:, i + n, :]) for n in range(2)]
+                    quantise_w(group_w(turned), i // 2)
 
                 tv_ps = sums.tile([P, N_TILE], F32, tag="sum")
                 mx_group(
                     nc, tv_ps[:],
-                    [(view(src_q, c, block(i)), view(theta_k_q, c, half(h))) for c in range(PASSES)],
+                    [(src_rows(i, c), view(theta_k_q, c, half(h))) for c in range(PASSES)],
                 )
                 nc.scalar.copy(
                     out=train_view_sb[:, i, half(h)].rearrange("p (u q e) -> p u q e", u=2, e=2),
@@ -210,13 +234,13 @@ def tile_tttinner_pa_kernel(tc, src, theta_k, theta_v, W, b, out_0, out_1):
                     out=train_view_blocks[:, i, half(h)], in_=train_view_sb[:, i, half(h)]
                 )
 
-                tv_flipped = sums.tile([P, PACK, P], F32, tag="sum")
+                tv_turned = sums.tile([P, PACK, P], F32, tag="sum")
                 for t in range(PACK):
                     u, e = divmod(t, 2)
                     mx_group(
-                        nc, tv_flipped[:, t, :],
+                        nc, tv_turned[:, t, :],
                         [
-                            (view(theta_k_q, c, block(PACK * h + 2 * e + u)), view(src_q, c, block(i)))
+                            (view(theta_k_q, c, block(PACK * h + 2 * e + u)), src_rows(i, c))
                             for c in range(PASSES)
                         ],
                     )
@@ -226,31 +250,30 @@ def tile_tttinner_pa_kernel(tc, src, theta_k, theta_v, W, b, out_0, out_1):
                     if step % 2 == 0:
                         piece_grouped = regroup(g, hp)
                     else:
-                        quantise_theta(piece_grouped, op, g, hp)
-                if i > 0:
-                    quantise_train_view(tv_grouped, h, i - 1)
-                tv_grouped = stage.tile([P, P * PACK], BF16, align_bytes=64, tag="tv_grouped")
+                        quantise(view(op, g, half(hp)), piece_grouped[:])
+                if step > 0 and i % 2 == 0:
+                    quantise(view(train_view_q, (step - 2) // BLOCKS, pair((step - 2) % BLOCKS // 2)), tv_grouped[:])
+                if i % 2 == 0:
+                    tv_grouped = stage.tile([P, 2 * P * PACK], BF16, align_bytes=64, tag="tv_grouped")
                 nc.scalar.copy(
-                    out=tv_grouped[:].rearrange("p (r t) -> p r t", t=PACK),
-                    in_=tv_flipped[:].rearrange("p t r -> p r t"),
+                    out=tv_grouped[:].rearrange("p (n r t) -> p n r t", n=2, t=PACK)[:, i % 2],
+                    in_=tv_turned[:].rearrange("p t r -> p r t"),
                 )
                 if h == 1:
-                    add_bias(i, 0)
-            quantise_train_view(tv_grouped, h, BLOCKS - 1)
+                    add_bias(i, 0, nc.vector)
+        quantise(view(train_view_q, 1, pair(BLOCKS // 2 - 1)), tv_grouped[:])
 
-        add_bias(0, 1)
+        add_bias(0, 1, nc.gpsimd)
         for i in range(BLOCKS):
             for h in range(HALVES):
                 err_ps = sums.tile([P, N_TILE], F32, tag="sum")
                 mx_group(
                     nc, err_ps[:],
-                    [(view(src_q, c, block(i)), view(minus_theta_v_q, c, half(h))) for c in range(PASSES)]
+                    [(src_rows(i, c), view(minus_theta_v_q, c, half(h))) for c in range(PASSES)]
                     + [(view(train_view_q, g, block(i)), view(w_q, g, half(h))) for g in range(PASSES)],
                 )
-                err_sb = results.tile([P, N_TILE], F32)
-                nc.vector.tensor_tensor(
-                    out=err_sb[:], in0=err_ps[:], in1=train_view_sb[:, i, half(h)], op=ADD
-                )
-                nc.sync.dma_start(out=err_blocks[:, i, half(h)], in_=err_sb[:])
                 if h == 0 and i + 1 < BLOCKS:
-                    add_bias(i + 1, 1)
+                    add_bias(i + 1, 1, nc.gpsimd)
+                err_sb = results.tile([P, N_TILE], F32)
+                nc.vector.tensor_tensor(out=err_sb[:], in0=err_ps[:], in1=biased[i, h], op=ADD)
+                nc.sync.dma_start(out=err_blocks[:, i, half(h)], in_=err_sb[:])

@@ -81,8 +81,14 @@ def tile_tttinner_pa_kernel(tc, src, theta_k, theta_v, W, b, out_0, out_1):
         make_identity(nc, identity[:])
         bias_row = const.tile([P, D], BF16)
         nc.gpsimd.memset(bias_row[:], 0.0)
-        ones = const.tile([P, P], BF16)
-        nc.gpsimd.memset(ones[:], 1.0)
+        ones = const.tile([P, N_TILE], BF16)
+        nc.vector.memset(ones[:], 1.0)
+
+        warm_up = sums.tile([P, N_TILE], F32, tag="sum", name="warm_up")
+
+        def keep_busy(matmuls):
+            for n in range(matmuls):
+                nc.tensor.matmul(out=warm_up[:], lhsT=ones[:, :P], rhs=ones[:], start=True, stop=True)
 
         for g in range(PASSES):
             load_theta(theta_k, half(0), g, theta_k_sb[:, 0, g])
@@ -179,7 +185,7 @@ def tile_tttinner_pa_kernel(tc, src, theta_k, theta_v, W, b, out_0, out_1):
             for h in range(HALVES):
                 bias_ps = sums.tile([P, N_TILE], F32, tag="sum")
                 nc.tensor.matmul(
-                    out=bias_ps[:], lhsT=ones[:], rhs=bias_row[:, half(h)], start=True, stop=True
+                    out=bias_ps[:], lhsT=ones[:, :P], rhs=bias_row[:, half(h)], start=True, stop=True
                 )
                 copies(out=bias_sb[:, half(h)], in_=bias_ps[:])
 
@@ -199,9 +205,11 @@ def tile_tttinner_pa_kernel(tc, src, theta_k, theta_v, W, b, out_0, out_1):
         theta_grouped = [regroup_theta_k(g, 0) for g in range(PASSES)]
         for g in range(PASSES):
             quantise(view(theta_k_q, g, half(0)), theta_grouped[g][:])
+        keep_busy(10)
         turned = [turn(src_sb[:, i, :]) for i in range(2)]
         for i in range(2):
             quantise_src(group_src(turned[i]), i)
+        keep_busy(3)
         spread_bias(nc.vector.tensor_copy)
 
 

@@ -139,9 +139,9 @@ def tile_tttinner_pa_kernel(tc, src, theta_k, theta_v, W, b, out_0, out_1):
                     )
             return turned
 
-        def group_src(turned):
+        def group_src(turned, copy):
             grouped = stage.tile([P, PASSES * P * PACK], BF16, align_bytes=64, tag="src_grouped")
-            nc.scalar.copy(
+            copy(
                 out=grouped[:].bitcast(F32).rearrange("p (g r u) -> p g r u", g=PASSES, u=2),
                 in_=turned[:].rearrange("p g u r -> p g r u"),
             )
@@ -151,11 +151,11 @@ def tile_tttinner_pa_kernel(tc, src, theta_k, theta_v, W, b, out_0, out_1):
             words, scales = src_q[0][:, i], src_q[1][:, i]
             quantise((words.rearrange("p g r -> p (g r)"), scales.rearrange("p g r -> p (g r)")), grouped[:])
 
-        def group_w(turned):
+        def group_w(turned, copies):
             grouped = stage.tile([P, PASSES * 2 * P * PACK], BF16, align_bytes=64, tag="w_grouped")
             words = grouped[:].bitcast(F32).rearrange("p (g n r u) -> p n g r u", g=PASSES, n=2, u=2)
             for n in range(2):
-                nc.scalar.copy(out=words[:, n], in_=turned[n][:].rearrange("p g u r -> p g r u"))
+                copies[n](out=words[:, n], in_=turned[n][:].rearrange("p g u r -> p g r u"))
             return grouped
 
         def quantise_w(grouped, j):
@@ -170,12 +170,12 @@ def tile_tttinner_pa_kernel(tc, src, theta_k, theta_v, W, b, out_0, out_1):
             )
             return grouped
 
-        def regroup_minus_theta_v(g, h):
+        def regroup_minus_theta_v(g, h, engine_mul):
             grouped = stage.tile([P, N_TILE * PACK], BF16, align_bytes=64, tag="theta_grouped")
-            nc.vector.tensor_scalar_mul(
-                out=grouped[:].rearrange("p (c i t) -> p c t i", i=4, t=PACK),
-                in0=theta_v_sb[:, g, :, half(h)].rearrange("p t (c i) -> p c t i", i=4),
-                scalar1=-1.0,
+            engine_mul(
+                grouped[:].rearrange("p (c i t) -> p c t i", i=4, t=PACK),
+                theta_v_sb[:, g, :, half(h)].rearrange("p t (c i) -> p c t i", i=4),
+                -1.0,
             )
             return grouped
 
@@ -193,10 +193,7 @@ def tile_tttinner_pa_kernel(tc, src, theta_k, theta_v, W, b, out_0, out_1):
         biased = {}
 
         def add_bias(i, h, engine):
-            if h == 0:
-                with_bias = train_view_sb[:, i, half(0)]
-            else:
-                with_bias = results.tile([P, N_TILE], F32, bufs=4, name="with_bias")[:]
+            with_bias = results.tile([P, N_TILE], F32, bufs=10, name="with_bias")[:]
             engine.tensor_tensor(
                 out=with_bias, in0=train_view_sb[:, i, half(h)], in1=bias_sb[:, half(h)], op=ADD
             )
@@ -208,26 +205,27 @@ def tile_tttinner_pa_kernel(tc, src, theta_k, theta_v, W, b, out_0, out_1):
         keep_busy(10)
         turned = [turn(src_sb[:, i, :]) for i in range(2)]
         for i in range(2):
-            quantise_src(group_src(turned[i]), i)
+            quantise_src(group_src(turned[i], nc.scalar.copy), i)
         keep_busy(3)
         spread_bias(nc.vector.tensor_copy)
 
 
         later_pieces = [(regroup_theta_k, theta_k_q, g, 1) for g in range(PASSES)] + [
-            (regroup_minus_theta_v, minus_theta_v_q, g, h)
+            (lambda g, h: regroup_minus_theta_v(g, h, nc.vector.tensor_scalar_mul), minus_theta_v_q, g, 0)
             for g in range(PASSES)
-            for h in range(HALVES)
         ]
 
         for h in range(HALVES):
             for i in range(BLOCKS):
+                step = h * BLOCKS + i
                 if i % 2 == 0 and h == 0 and i + 2 < BLOCKS:
                     turned = [turn(src_sb[:, i + 2 + n, :]) for n in range(2)]
+                    grouped = [group_src(turned[0], nc.scalar.copy), group_src(turned[1], nc.vector.tensor_copy)]
                     for n in range(2):
-                        quantise_src(group_src(turned[n]), i + 2 + n)
-                if i % 2 == 0 and h == 1:
-                    turned = [turn(w_sb[:, i + n, :]) for n in range(2)]
-                    quantise_w(group_w(turned), i // 2)
+                        quantise_src(grouped[n], i + 2 + n)
+                if h == 1 and i in (0, 2):
+                    turned = [turn(w_sb[:, (0, 2).index(i) * 2 + n, :]) for n in range(2)]
+                    quantise_w(group_w(turned, [nc.scalar.copy, nc.vector.tensor_copy]), (0, 2).index(i))
 
                 tv_ps = sums.tile([P, N_TILE], F32, tag="sum")
                 mx_group(
@@ -252,13 +250,11 @@ def tile_tttinner_pa_kernel(tc, src, theta_k, theta_v, W, b, out_0, out_1):
                             for c in range(PASSES)
                         ],
                     )
-                step = h * BLOCKS + i
-                if step // 2 < len(later_pieces):
-                    regroup, op, g, hp = later_pieces[step // 2]
-                    if step % 2 == 0:
-                        piece_grouped = regroup(g, hp)
-                    else:
-                        quantise(view(op, g, half(hp)), piece_grouped[:])
+                if step in (0, 2, 6, 10):
+                    regroup, op, g, hp = later_pieces[(0, 2, 6, 10).index(step)]
+                    piece_grouped = regroup(g, hp)
+                if step - 1 in (0, 2, 6, 10):
+                    quantise(view(op, g, half(hp)), piece_grouped[:])
                 if step > 0 and i % 2 == 0:
                     quantise(view(train_view_q, (step - 2) // BLOCKS, pair((step - 2) % BLOCKS // 2)), tv_grouped[:])
                 if i % 2 == 0:
@@ -271,17 +267,28 @@ def tile_tttinner_pa_kernel(tc, src, theta_k, theta_v, W, b, out_0, out_1):
                     add_bias(i, 0, nc.vector)
         quantise(view(train_view_q, 1, pair(BLOCKS // 2 - 1)), tv_grouped[:])
 
-        add_bias(0, 1, nc.gpsimd)
-        for i in range(BLOCKS):
-            for h in range(HALVES):
+        pieces = []
+        for h in range(HALVES):
+            for i in range(BLOCKS):
+                if h == 0 and i in (0, 2):
+                    turned = [turn(w_sb[:, 4 + i + n, :]) for n in range(2)]
+                    w_grouped = group_w(turned, [nc.scalar.copy, nc.scalar.copy])
+                    pieces.append(regroup_minus_theta_v(i // 2, 1, [nc.scalar.mul, nc.vector.tensor_scalar_mul][i // 2]))
                 err_ps = sums.tile([P, N_TILE], F32, tag="sum")
                 mx_group(
                     nc, err_ps[:],
                     [(src_rows(i, c), view(minus_theta_v_q, c, half(h))) for c in range(PASSES)]
                     + [(view(train_view_q, g, block(i)), view(w_q, g, half(h))) for g in range(PASSES)],
                 )
-                if h == 0 and i + 1 < BLOCKS:
-                    add_bias(i + 1, 1, nc.gpsimd)
                 err_sb = results.tile([P, N_TILE], F32)
                 nc.vector.tensor_tensor(out=err_sb[:], in0=err_ps[:], in1=biased[i, h], op=ADD)
                 nc.sync.dma_start(out=err_blocks[:, i, half(h)], in_=err_sb[:])
+                if h == 0 and i in (0, 2):
+                    quantise_w(w_grouped, 2 + i // 2)
+                if h == 0 and i in (4, 5):
+                    g = i - 4
+                    quantise(view(minus_theta_v_q, g, half(1)), pieces[g][:])
+                if h == 0 and i % 2 == 0:
+                    add_bias(i // 2, 1, nc.gpsimd)
+                if h == 1 and i % 2 == 0:
+                    add_bias(4 + i // 2, 1, nc.gpsimd)

@@ -193,7 +193,7 @@ def tile_tttinner_pa_kernel(tc, src, theta_k, theta_v, W, b, out_0, out_1):
         biased = {}
 
         def add_bias(i, h, engine):
-            with_bias = results.tile([P, N_TILE], F32, bufs=10, name="with_bias")[:]
+            with_bias = results.tile([P, N_TILE], F32, bufs=BLOCKS if h == 0 else 4, name="with_bias_%d" % h)[:]
             engine.tensor_tensor(
                 out=with_bias, in0=train_view_sb[:, i, half(h)], in1=bias_sb[:, half(h)], op=ADD
             )
@@ -274,21 +274,30 @@ def tile_tttinner_pa_kernel(tc, src, theta_k, theta_v, W, b, out_0, out_1):
                     turned = [turn(w_sb[:, 4 + i + n, :]) for n in range(2)]
                     w_grouped = group_w(turned, [nc.scalar.copy, nc.scalar.copy])
                     pieces.append(regroup_minus_theta_v(i // 2, 1, [nc.scalar.mul, nc.vector.tensor_scalar_mul][i // 2]))
-                err_ps = sums.tile([P, N_TILE], F32, tag="sum")
-                mx_group(
-                    nc, err_ps[:],
-                    [(src_rows(i, c), view(minus_theta_v_q, c, half(h))) for c in range(PASSES)]
-                    + [(view(train_view_q, g, block(i)), view(w_q, g, half(h))) for g in range(PASSES)],
-                )
-                err_sb = results.tile([P, N_TILE], F32)
-                nc.vector.tensor_tensor(out=err_sb[:], in0=err_ps[:], in1=biased[i, h], op=ADD)
-                nc.sync.dma_start(out=err_blocks[:, i, half(h)], in_=err_sb[:])
+                parts = 2 if (i, h) == (BLOCKS - 1, HALVES - 1) else 1
+                width = N_TILE // parts
+                for part in range(parts):
+                    columns = slice(h * N_TILE + part * width, h * N_TILE + (part + 1) * width)
+                    err_ps = sums.tile([P, width], F32, tag="sum")
+                    mx_group(
+                        nc, err_ps[:],
+                        [(src_rows(i, c), view(minus_theta_v_q, c, columns)) for c in range(PASSES)]
+                        + [(view(train_view_q, g, block(i)), view(w_q, g, columns)) for g in range(PASSES)],
+                    )
+                    err_sb = results.tile([P, width], F32, name="err_sb")
+                    nc.vector.tensor_tensor(
+                        out=err_sb[:],
+                        in0=err_ps[:],
+                        in1=biased[i, h][:, part * width : (part + 1) * width],
+                        op=ADD,
+                    )
+                    nc.sync.dma_start(out=err_blocks[:, i, columns], in_=err_sb[:])
                 if h == 0 and i in (0, 2):
                     quantise_w(w_grouped, 2 + i // 2)
                 if h == 0 and i in (4, 5):
                     g = i - 4
                     quantise(view(minus_theta_v_q, g, half(1)), pieces[g][:])
-                if h == 0 and i % 2 == 0:
-                    add_bias(i // 2, 1, nc.gpsimd)
-                if h == 1 and i % 2 == 0:
-                    add_bias(4 + i // 2, 1, nc.gpsimd)
+                if h == 0 and i >= BLOCKS - 3:
+                    add_bias(i - BLOCKS + 3, 1, nc.vector)
+                if h == 1 and i + 3 < BLOCKS:
+                    add_bias(i + 3, 1, nc.gpsimd)

@@ -139,9 +139,9 @@ def tile_tttinner_pa_kernel(tc, src, theta_k, theta_v, W, b, out_0, out_1):
                     )
             return turned
 
-        def group_src(turned, copy):
+        def group_src(turned):
             grouped = stage.tile([P, PASSES * P * PACK], BF16, align_bytes=64, tag="src_grouped")
-            copy(
+            nc.scalar.copy(
                 out=grouped[:].bitcast(F32).rearrange("p (g r u) -> p g r u", g=PASSES, u=2),
                 in_=turned[:].rearrange("p g u r -> p g r u"),
             )
@@ -151,11 +151,11 @@ def tile_tttinner_pa_kernel(tc, src, theta_k, theta_v, W, b, out_0, out_1):
             words, scales = src_q[0][:, i], src_q[1][:, i]
             quantise((words.rearrange("p g r -> p (g r)"), scales.rearrange("p g r -> p (g r)")), grouped[:])
 
-        def group_w(turned, copies):
-            grouped = stage.tile([P, PASSES * 2 * P * PACK], BF16, align_bytes=64, tag="w_grouped")
+        def group_w(turned):
+            grouped = stage.tile([P, PASSES * 2 * P * PACK], BF16, align_bytes=64, tag="w_grouped", bufs=2)
             words = grouped[:].bitcast(F32).rearrange("p (g n r u) -> p n g r u", g=PASSES, n=2, u=2)
             for n in range(2):
-                copies[n](out=words[:, n], in_=turned[n][:].rearrange("p g u r -> p g r u"))
+                nc.scalar.copy(out=words[:, n], in_=turned[n][:].rearrange("p g u r -> p g r u"))
             return grouped
 
         def quantise_w(grouped, j):
@@ -163,19 +163,19 @@ def tile_tttinner_pa_kernel(tc, src, theta_k, theta_v, W, b, out_0, out_1):
                 quantise(view(w_q, g, pair(j)), grouped[:, 2 * g * K_PASS : 2 * (g + 1) * K_PASS])
 
         def regroup_theta_k(g, h):
-            grouped = stage.tile([P, N_TILE * PACK], BF16, align_bytes=64, tag="theta_grouped")
+            grouped = stage.tile([P, N_TILE * PACK], BF16, align_bytes=64, tag="theta_grouped", bufs=3)
             nc.vector.tensor_copy(
                 out=grouped[:].rearrange("p (e c t) -> p e c t", e=2, t=PACK),
                 in_=theta_k_sb[:, h, g].rearrange("p t (c e) -> p e c t", e=2),
             )
             return grouped
 
-        def regroup_minus_theta_v(g, h, engine_mul):
-            grouped = stage.tile([P, N_TILE * PACK], BF16, align_bytes=64, tag="theta_grouped")
-            engine_mul(
-                grouped[:].rearrange("p (c i t) -> p c t i", i=4, t=PACK),
-                theta_v_sb[:, g, :, half(h)].rearrange("p t (c i) -> p c t i", i=4),
-                -1.0,
+        def regroup_minus_theta_v(g, h):
+            grouped = stage.tile([P, N_TILE * PACK], BF16, align_bytes=64, tag="theta_grouped", bufs=3)
+            nc.vector.tensor_scalar_mul(
+                out=grouped[:].rearrange("p (c i t) -> p c t i", i=4, t=PACK),
+                in0=theta_v_sb[:, g, :, half(h)].rearrange("p t (c i) -> p c t i", i=4),
+                scalar1=-1.0,
             )
             return grouped
 
@@ -193,7 +193,7 @@ def tile_tttinner_pa_kernel(tc, src, theta_k, theta_v, W, b, out_0, out_1):
         biased = {}
 
         def add_bias(i, h, engine):
-            with_bias = results.tile([P, N_TILE], F32, bufs=BLOCKS if h == 0 else 4, name="with_bias_%d" % h)[:]
+            with_bias = results.tile([P, N_TILE], F32, bufs=(BLOCKS if h == 0 else 6), name="with_bias_%d" % h)[:]
             engine.tensor_tensor(
                 out=with_bias, in0=train_view_sb[:, i, half(h)], in1=bias_sb[:, half(h)], op=ADD
             )
@@ -202,78 +202,131 @@ def tile_tttinner_pa_kernel(tc, src, theta_k, theta_v, W, b, out_0, out_1):
         theta_grouped = [regroup_theta_k(g, 0) for g in range(PASSES)]
         for g in range(PASSES):
             quantise(view(theta_k_q, g, half(0)), theta_grouped[g][:])
-        keep_busy(10)
+        keep_busy(6)
         turned = [turn(src_sb[:, i, :]) for i in range(2)]
         for i in range(2):
-            quantise_src(group_src(turned[i], nc.scalar.copy), i)
-        keep_busy(3)
+            quantise_src(group_src(turned[i]), i)
+        keep_busy(1)
         spread_bias(nc.vector.tensor_copy)
 
 
         later_pieces = [(regroup_theta_k, theta_k_q, g, 1) for g in range(PASSES)] + [
-            (lambda g, h: regroup_minus_theta_v(g, h, nc.vector.tensor_scalar_mul), minus_theta_v_q, g, 0)
+            (regroup_minus_theta_v, minus_theta_v_q, g, 0)
             for g in range(PASSES)
-        ]
+        ] + [(regroup_minus_theta_v, minus_theta_v_q, g, 1) for g in range(PASSES)]
 
-        for h in range(HALVES):
-            for i in range(BLOCKS):
-                step = h * BLOCKS + i
-                if i % 2 == 0 and h == 0 and i + 2 < BLOCKS:
-                    turned = [turn(src_sb[:, i + 2 + n, :]) for n in range(2)]
-                    grouped = [group_src(turned[0], nc.scalar.copy), group_src(turned[1], nc.vector.tensor_copy)]
-                    for n in range(2):
-                        quantise_src(grouped[n], i + 2 + n)
-                if h == 1 and i in (0, 2):
-                    turned = [turn(w_sb[:, (0, 2).index(i) * 2 + n, :]) for n in range(2)]
-                    quantise_w(group_w(turned, [nc.scalar.copy, nc.vector.tensor_copy]), (0, 2).index(i))
+        piece_steps = [0, 2, 5, 7, 17, 19]
 
-                tv_ps = sums.tile([P, N_TILE], F32, tag="sum")
-                mx_group(
-                    nc, tv_ps[:],
-                    [(src_rows(i, c), view(theta_k_q, c, half(h))) for c in range(PASSES)],
-                )
-                nc.scalar.copy(
-                    out=train_view_sb[:, i, half(h)].rearrange("p (u q e) -> p u q e", u=2, e=2),
-                    in_=tv_ps[:].rearrange("p (e u q) -> p u q e", e=2, u=2),
-                )
-                nc.sync.dma_start(
-                    out=train_view_blocks[:, i, half(h)], in_=train_view_sb[:, i, half(h)]
-                )
+        rounded = {}
 
-                tv_turned = sums.tile([P, PACK, P], F32, tag="sum")
-                for t in range(PACK):
-                    u, e = divmod(t, 2)
-                    mx_group(
-                        nc, tv_turned[:, t, :],
-                        [
-                            (view(theta_k_q, c, block(PACK * h + 2 * e + u)), src_rows(i, c))
-                            for c in range(PASSES)
-                        ],
+        def round_train_view(tv_ps, i, copy):
+            rounded[i] = stage.tile([P, N_TILE], BF16, bufs=6, name="rounded")
+            copy(
+                out=rounded[i][:].rearrange("p (u q e) -> p u q e", u=2, e=2),
+                in_=tv_ps[:].rearrange("p (e u q) -> p u q e", e=2, u=2),
+            )
+
+        def turn_train_view(j):
+            turned = psum.tile([P, 2, 2, P], F32, tag="turned")
+            for n in range(2):
+                words = rounded[2 * j + n][:].bitcast(F32)
+                for u in range(2):
+                    nc.tensor.transpose(
+                        out=turned[:, n, u, :], in_=words[:, u * P : (u + 1) * P], identity=identity[:]
                     )
-                if step in (0, 2, 6, 10):
-                    regroup, op, g, hp = later_pieces[(0, 2, 6, 10).index(step)]
-                    piece_grouped = regroup(g, hp)
-                if step - 1 in (0, 2, 6, 10):
-                    quantise(view(op, g, half(hp)), piece_grouped[:])
-                if step > 0 and i % 2 == 0:
-                    quantise(view(train_view_q, (step - 2) // BLOCKS, pair((step - 2) % BLOCKS // 2)), tv_grouped[:])
-                if i % 2 == 0:
-                    tv_grouped = stage.tile([P, 2 * P * PACK], BF16, align_bytes=64, tag="tv_grouped")
-                nc.scalar.copy(
-                    out=tv_grouped[:].rearrange("p (n r t) -> p n r t", n=2, t=PACK)[:, i % 2],
-                    in_=tv_turned[:].rearrange("p t r -> p r t"),
-                )
-                if h == 1:
-                    add_bias(i, 0, nc.vector)
-        quantise(view(train_view_q, 1, pair(BLOCKS // 2 - 1)), tv_grouped[:])
+            return turned
 
-        pieces = []
+        def group_train_view(turned):
+            grouped = stage.tile([P, 2 * P * PACK], BF16, align_bytes=64, tag="tv_grouped")
+            nc.scalar.copy(
+                out=grouped[:].bitcast(F32).rearrange("p (n r u) -> p n r u", n=2, u=2),
+                in_=turned[:].rearrange("p n u r -> p n r u"),
+            )
+            return grouped
+
+        def train_view(i, h, copy):
+            tv_ps = sums.tile([P, N_TILE], F32, tag="sum")
+            mx_group(
+                nc, tv_ps[:],
+                [(src_rows(i, c), view(theta_k_q, c, half(h))) for c in range(PASSES)],
+            )
+            copy(
+                out=train_view_sb[:, i, half(h)].rearrange("p (u q e) -> p u q e", u=2, e=2),
+                in_=tv_ps[:].rearrange("p (e u q) -> p u q e", e=2, u=2),
+            )
+            nc.sync.dma_start(
+                out=train_view_blocks[:, i, half(h)], in_=train_view_sb[:, i, half(h)]
+            )
+            return tv_ps
+
+        def theta_piece(step):
+            if step in piece_steps:
+                regroup, op, g, hp = later_pieces[piece_steps.index(step)]
+                pieces[step] = regroup(g, hp)
+            if step - 1 in pieces:
+                regroup, op, g, hp = later_pieces[piece_steps.index(step - 1)]
+                quantise(view(op, g, half(hp)), pieces[step - 1][:])
+
+        pieces = {}
+        for i in range(BLOCKS):
+            if i % 2 == 0 and i + 2 < BLOCKS:
+                turned = [turn(src_sb[:, i + 2 + n, :]) for n in range(2)]
+                for n in range(2):
+                    quantise_src(group_src(turned[n]), i + 2 + n)
+            train_view(i, 0, nc.scalar.copy)
+            tv_turned = sums.tile([P, PACK, P], F32, tag="sum")
+            for t in range(PACK):
+                u, e = divmod(t, 2)
+                mx_group(
+                    nc, tv_turned[:, t, :],
+                    [
+                        (view(theta_k_q, c, block(2 * e + u)), src_rows(i, c))
+                        for c in range(PASSES)
+                    ],
+                )
+            theta_piece(i)
+            if i % 2 == 0:
+                if i > 0:
+                    quantise(view(train_view_q, 0, pair(i // 2 - 1)), tv_grouped[:])
+                tv_grouped = stage.tile([P, 2 * P * PACK], BF16, align_bytes=64, tag="tv_grouped")
+            nc.scalar.copy(
+                out=tv_grouped[:].rearrange("p (n r t) -> p n r t", n=2, t=PACK)[:, i % 2],
+                in_=tv_turned[:].rearrange("p t r -> p r t"),
+            )
+        quantise(view(train_view_q, 0, pair(BLOCKS // 2 - 1)), tv_grouped[:])
+
+        def turn_run(j, w_pair):
+            tv = None if j is None else turn_train_view(j)
+            w = None if w_pair is None else [turn(w_sb[:, 2 * w_pair + n, :]) for n in range(2)]
+            return (
+                None if tv is None else group_train_view(tv),
+                None if w is None else group_w(w),
+            )
+
+        def quantise_run(j, w_pair, tv, w):
+            if tv is not None:
+                quantise(view(train_view_q, 1, pair(j)), tv[:])
+            if w is not None:
+                quantise_w(w, w_pair)
+
+        runs = {0: (None, 0), 2: (None, 1), 4: (0, None), 6: (1, None)}
+        for i in range(BLOCKS):
+            if i in runs:
+                run = turn_run(*runs[i])
+            copy = nc.vector.tensor_copy if i % 2 else nc.scalar.copy
+            round_train_view(train_view(i, 1, copy), i, copy)
+            theta_piece(BLOCKS + i)
+            if i in runs:
+                quantise_run(*runs[i], *run)
+            add_bias(i, 0, nc.gpsimd)
+
+        runs = {0: (2, 2), 2: (3, 3)}
         for h in range(HALVES):
             for i in range(BLOCKS):
-                if h == 0 and i in (0, 2):
-                    turned = [turn(w_sb[:, 4 + i + n, :]) for n in range(2)]
-                    w_grouped = group_w(turned, [nc.scalar.copy, nc.scalar.copy])
-                    pieces.append(regroup_minus_theta_v(i // 2, 1, [nc.scalar.mul, nc.vector.tensor_scalar_mul][i // 2]))
+                if h == 0 and i in runs:
+                    run = turn_run(*runs[i])
+                if h == 0:
+                    theta_piece(2 * BLOCKS + i)
                 parts = 2 if (i, h) == (BLOCKS - 1, HALVES - 1) else 1
                 width = N_TILE // parts
                 for part in range(parts):
@@ -292,11 +345,8 @@ def tile_tttinner_pa_kernel(tc, src, theta_k, theta_v, W, b, out_0, out_1):
                         op=ADD,
                     )
                     nc.sync.dma_start(out=err_blocks[:, i, columns], in_=err_sb[:])
-                if h == 0 and i in (0, 2):
-                    quantise_w(w_grouped, 2 + i // 2)
-                if h == 0 and i in (4, 5):
-                    g = i - 4
-                    quantise(view(minus_theta_v_q, g, half(1)), pieces[g][:])
+                if h == 0 and i in runs:
+                    quantise_run(*runs[i], *run)
                 if h == 0 and i >= BLOCKS - 3:
                     add_bias(i - BLOCKS + 3, 1, nc.vector)
                 if h == 1 and i + 3 < BLOCKS:

@@ -44,8 +44,8 @@ def tile_tttinner_pa_kernel(tc, src, theta_k, theta_v, W, b, out_0, out_1):
         keep = ctx.enter_context(tc.tile_pool(name="keep", bufs=1))
         stage = ctx.enter_context(tc.tile_pool(name="stage", bufs=4))
         results = ctx.enter_context(tc.tile_pool(name="results", bufs=6))
-        psum = ctx.enter_context(tc.psum_pool(name="psum", bufs=2))
-        sums = ctx.enter_context(tc.psum_pool(name="sums", bufs=6))
+        psum = ctx.enter_context(tc.psum_pool(name="psum", bufs=3))
+        sums = ctx.enter_context(tc.psum_pool(name="sums", bufs=5))
         ctx.enter_context(tc.manual_schedule())
 
         src_blocks = src.rearrange("(p j) d -> p j d", j=BLOCKS)
@@ -193,7 +193,7 @@ def tile_tttinner_pa_kernel(tc, src, theta_k, theta_v, W, b, out_0, out_1):
         biased = {}
 
         def add_bias(i, h, engine):
-            with_bias = results.tile([P, N_TILE], F32, bufs=(BLOCKS if h == 0 else 6), name="with_bias_%d" % h)[:]
+            with_bias = results.tile([P, N_TILE], F32, bufs=BLOCKS if h == 0 else 3, name="with_bias_%d" % h)[:]
             engine.tensor_tensor(
                 out=with_bias, in0=train_view_sb[:, i, half(h)], in1=bias_sb[:, half(h)], op=ADD
             )
@@ -215,7 +215,7 @@ def tile_tttinner_pa_kernel(tc, src, theta_k, theta_v, W, b, out_0, out_1):
             for g in range(PASSES)
         ] + [(regroup_minus_theta_v, minus_theta_v_q, g, 1) for g in range(PASSES)]
 
-        piece_steps = [0, 2, 5, 7, 17, 19]
+        piece_steps = [0, 2, 4, 6, 9, 11]
 
         rounded = {}
 
@@ -313,12 +313,11 @@ def tile_tttinner_pa_kernel(tc, src, theta_k, theta_v, W, b, out_0, out_1):
         for i in range(BLOCKS):
             if i in runs:
                 run = turn_run(*runs[i])
-            copy = nc.vector.tensor_copy if i % 2 else nc.scalar.copy
+            copy = nc.vector.tensor_copy if i % 4 == 1 else nc.scalar.copy
             round_train_view(train_view(i, 1, copy), i, copy)
-            theta_piece(BLOCKS + i)
-            if i in runs:
-                quantise_run(*runs[i], *run)
-            add_bias(i, 0, nc.gpsimd)
+            if i - 1 in runs:
+                quantise_run(*runs[i - 1], *run)
+            add_bias(i, 0, nc.vector)
 
         runs = {0: (2, 2), 2: (3, 3)}
         for h in range(HALVES):
@@ -326,7 +325,7 @@ def tile_tttinner_pa_kernel(tc, src, theta_k, theta_v, W, b, out_0, out_1):
                 if h == 0 and i in runs:
                     run = turn_run(*runs[i])
                 if h == 0:
-                    theta_piece(2 * BLOCKS + i)
+                    theta_piece(BLOCKS + i)
                 parts = 2 if (i, h) == (BLOCKS - 1, HALVES - 1) else 1
                 width = N_TILE // parts
                 for part in range(parts):
@@ -345,8 +344,8 @@ def tile_tttinner_pa_kernel(tc, src, theta_k, theta_v, W, b, out_0, out_1):
                         op=ADD,
                     )
                     nc.sync.dma_start(out=err_blocks[:, i, columns], in_=err_sb[:])
-                if h == 0 and i in runs:
-                    quantise_run(*runs[i], *run)
+                if h == 0 and i - 1 in runs:
+                    quantise_run(*runs[i - 1], *run)
                 if h == 0 and i >= BLOCKS - 3:
                     add_bias(i - BLOCKS + 3, 1, nc.vector)
                 if h == 1 and i + 3 < BLOCKS:

from contextlib import ExitStack

import concourse.mybir as mybir
from concourse.masks import make_identity

F32 = mybir.dt.float32
BF16 = mybir.dt.bfloat16
U32 = mybir.dt.uint32
U8 = mybir.dt.uint8
FP8X4 = mybir.dt.float8_e4m3fn_x4
ADD = mybir.AluOpType.add

P = 128
PACK = 4
K_PASS = P * PACK
T = 1024
D = 1024
PASSES = D // K_PASS
BLOCKS = T // P
N_TILE = 512
HALVES = D // N_TILE

FLOPS = 3 * 2 * T * D * D


def mx_group(nc, out, products):
    last = len(products) - 1
    for n, (stationary, moving) in enumerate(products):
        nc.tensor.matmul_mx(
            out=out,
            lhsT=stationary[0].bitcast(FP8X4),
            lhsT_scale=stationary[1],
            rhs=moving[0].bitcast(FP8X4),
            rhs_scale=moving[1],
            start=(n == 0),
            stop=(n == last),
        )


def tile_tttinner_pa_kernel(tc, src, theta_k, theta_v, W, b, out_0, out_1):
    nc = tc.nc
    with ExitStack() as ctx:
        const = ctx.enter_context(tc.tile_pool(name="const", bufs=1))
        keep = ctx.enter_context(tc.tile_pool(name="keep", bufs=1))
        stage = ctx.enter_context(tc.tile_pool(name="stage", bufs=4))
        results = ctx.enter_context(tc.tile_pool(name="results", bufs=6))
        psum = ctx.enter_context(tc.psum_pool(name="psum", bufs=3))
        sums = ctx.enter_context(tc.psum_pool(name="sums", bufs=5))
        ctx.enter_context(tc.manual_schedule())

        src_blocks = src.rearrange("(p j) d -> p j d", j=BLOCKS)
        train_view_blocks = out_0.rearrange("(p j) d -> p j d", j=BLOCKS)
        err_blocks = out_1.rearrange("(p j) d -> p j d", j=BLOCKS)

        src_sb = keep.tile([P, BLOCKS, D], BF16)
        w_sb = keep.tile([P, BLOCKS, D], BF16)
        theta_k_sb = keep.tile([P, HALVES, PASSES, PACK, N_TILE], BF16)
        theta_v_sb = keep.tile([P, PASSES, PACK, D], BF16)

        def half(h):
            return slice(h * N_TILE, (h + 1) * N_TILE)

        def block(i):
            return slice(i * P, (i + 1) * P)

        def pair(j):
            return slice(2 * j * P, (2 * j + 2) * P)

        def load_src(j, n):
            nc.sync.dma_start(out=src_sb[:, j : j + n, :], in_=src_blocks[:, j : j + n, :])

        def load_theta(theta, columns, g, out):
            for u in range(2):
                first = g * K_PASS + u * 2 * P
                nc.sync.dma_start(
                    out=out[:, 2 * u : 2 * u + 2, :],
                    in_=theta[first : first + 2 * P, columns].rearrange("(q e) c -> q e c", e=2),
                )

        identity = const.tile([P, P], F32)
        make_identity(nc, identity[:])
        bias_row = const.tile([P, D], BF16)
        nc.gpsimd.memset(bias_row[:], 0.0)
        ones = const.tile([P, N_TILE], BF16)
        nc.vector.memset(ones[:], 1.0)

        warm_up = sums.tile([P, N_TILE], F32, tag="sum", name="warm_up")

        def keep_busy(matmuls):
            for n in range(matmuls):
                nc.tensor.matmul(out=warm_up[:], lhsT=ones[:, :P], rhs=ones[:], start=True, stop=True)

        for g in range(PASSES):
            load_theta(theta_k, half(0), g, theta_k_sb[:, 0, g])
        load_src(0, 2)
        nc.sync.dma_start(out=bias_row[0:1, :], in_=b.rearrange("(o n) -> o n", o=1))
        for j in range(2, BLOCKS, 2):
            load_src(j, 2)
        for g in range(PASSES):
            load_theta(theta_k, half(1), g, theta_k_sb[:, 1, g])
        for g in range(PASSES):
            load_theta(theta_v, slice(0, D), g, theta_v_sb[:, g])
        for j in range(0, BLOCKS, 2):
            nc.sync.dma_start(
                out=w_sb[:, j : j + 2, :],
                in_=W[j * P : (j + 2) * P, :].rearrange("(j p) f -> p j f", p=P),
            )


        def operand(name, shape):
            words = keep.tile(shape, U32, align_bytes=64, name=name + "_words")
            scales = keep.tile(shape, U8, align_bytes=64, name=name + "_scales")
            return words, scales

        src_q = operand("src", [P, BLOCKS, PASSES, P])
        theta_k_q = operand("theta_k", [P, PASSES, D])
        minus_theta_v_q = operand("minus_theta_v", [P, PASSES, D])
        w_q = operand("w", [P, PASSES, D])
        train_view_q = operand("train_view", [P, PASSES, D])

        def view(op, g, columns):
            return op[0][:, g, columns], op[1][:, g, columns]

        def src_rows(i, g):
            return src_q[0][:, i, g, :], src_q[1][:, i, g, :]

        def quantise(operand_view, grouped):
            words, scales = operand_view
            nc.vector.quantize_mx(out=words.bitcast(FP8X4), scales=scales, in_=grouped)

        def turn(rows):
            words = rows.bitcast(F32)
            turned = psum.tile([P, PASSES, 2, P], F32, tag="turned")
            for g in range(PASSES):
                for u in range(2):
                    first = (2 * g + u) * P
                    nc.tensor.transpose(
                        out=turned[:, g, u, :], in_=words[:, first : first + P], identity=identity[:]
                    )
            return turned

        def group_src(turned):
            grouped = stage.tile([P, PASSES * P * PACK], BF16, align_bytes=64, tag="src_grouped")
            nc.scalar.copy(
                out=grouped[:].bitcast(F32).rearrange("p (g r u) -> p g r u", g=PASSES, u=2),
                in_=turned[:].rearrange("p g u r -> p g r u"),
            )
            return grouped

        def quantise_src(grouped, i):
            words, scales = src_q[0][:, i], src_q[1][:, i]
            quantise((words.rearrange("p g r -> p (g r)"), scales.rearrange("p g r -> p (g r)")), grouped[:])

        def group_w(turned):
            grouped = stage.tile([P, PASSES * 2 * P * PACK], BF16, align_bytes=64, tag="w_grouped", bufs=2)
            words = grouped[:].bitcast(F32).rearrange("p (g n r u) -> p n g r u", g=PASSES, n=2, u=2)
            for n in range(2):
                nc.scalar.copy(out=words[:, n], in_=turned[n][:].rearrange("p g u r -> p g r u"))
            return grouped

        def quantise_w(grouped, j):
            for g in range(PASSES):
                quantise(view(w_q, g, pair(j)), grouped[:, 2 * g * K_PASS : 2 * (g + 1) * K_PASS])

        def regroup_theta_k(g, h):
            grouped = stage.tile([P, N_TILE * PACK], BF16, align_bytes=64, tag="theta_grouped", bufs=3)
            nc.vector.tensor_copy(
                out=grouped[:].rearrange("p (e c t) -> p e c t", e=2, t=PACK),
                in_=theta_k_sb[:, h, g].rearrange("p t (c e) -> p e c t", e=2),
            )
            return grouped

        def regroup_minus_theta_v(g, h):
            grouped = stage.tile([P, N_TILE * PACK], BF16, align_bytes=64, tag="theta_grouped", bufs=3)
            nc.vector.tensor_scalar_mul(
                out=grouped[:].rearrange("p (c i t) -> p c t i", i=4, t=PACK),
                in0=theta_v_sb[:, g, :, half(h)].rearrange("p t (c i) -> p c t i", i=4),
                scalar1=-1.0,
            )
            return grouped

        bias_sb = const.tile([P, D], F32)

        def spread_bias(copies):
            for h in range(HALVES):
                bias_ps = sums.tile([P, N_TILE], F32, tag="sum")
                nc.tensor.matmul(
                    out=bias_ps[:], lhsT=ones[:, :P], rhs=bias_row[:, half(h)], start=True, stop=True
                )
                copies(out=bias_sb[:, half(h)], in_=bias_ps[:])

        train_view_sb = keep.tile([P, BLOCKS, D], F32)
        biased = {}

        def add_bias(i, h, engine):
            with_bias = results.tile([P, N_TILE], F32, bufs=BLOCKS if h == 0 else 3, name="with_bias_%d" % h)[:]
            engine.tensor_tensor(
                out=with_bias, in0=train_view_sb[:, i, half(h)], in1=bias_sb[:, half(h)], op=ADD
            )
            biased[i, h] = with_bias

        theta_grouped = [regroup_theta_k(g, 0) for g in range(PASSES)]
        for g in range(PASSES):
            quantise(view(theta_k_q, g, half(0)), theta_grouped[g][:])
        keep_busy(6)
        turned = [turn(src_sb[:, i, :]) for i in range(2)]
        for i in range(2):
            quantise_src(group_src(turned[i]), i)
        keep_busy(1)
        spread_bias(nc.vector.tensor_copy)


        later_pieces = [(regroup_theta_k, theta_k_q, g, 1) for g in range(PASSES)] + [
            (regroup_minus_theta_v, minus_theta_v_q, g, 0)
            for g in range(PASSES)
        ] + [(regroup_minus_theta_v, minus_theta_v_q, g, 1) for g in range(PASSES)]

        piece_steps = [0, 2, 4, 6, 9, 11]

        rounded = {}

        def round_train_view(tv_ps, i, copy):
            rounded[i] = stage.tile([P, N_TILE], BF16, bufs=6, name="rounded")
            copy(
                out=rounded[i][:].rearrange("p (u q e) -> p u q e", u=2, e=2),
                in_=tv_ps[:].rearrange("p (e u q) -> p u q e", e=2, u=2),
            )

        def turn_train_view(j):
            turned = psum.tile([P, 2, 2, P], F32, tag="turned")
            for n in range(2):
                words = rounded[2 * j + n][:].bitcast(F32)
                for u in range(2):
                    nc.tensor.transpose(
                        out=turned[:, n, u, :], in_=words[:, u * P : (u + 1) * P], identity=identity[:]
                    )
            return turned

        def group_train_view(turned):
            grouped = stage.tile([P, 2 * P * PACK], BF16, align_bytes=64, tag="tv_grouped")
            nc.scalar.copy(
                out=grouped[:].bitcast(F32).rearrange("p (n r u) -> p n r u", n=2, u=2),
                in_=turned[:].rearrange("p n u r -> p n r u"),
            )
            return grouped

        def train_view(i, h, copy):
            tv_ps = sums.tile([P, N_TILE], F32, tag="sum")
            mx_group(
                nc, tv_ps[:],
                [(src_rows(i, c), view(theta_k_q, c, half(h))) for c in range(PASSES)],
            )
            copy(
                out=train_view_sb[:, i, half(h)].rearrange("p (u q e) -> p u q e", u=2, e=2),
                in_=tv_ps[:].rearrange("p (e u q) -> p u q e", e=2, u=2),
            )
            nc.sync.dma_start(
                out=train_view_blocks[:, i, half(h)], in_=train_view_sb[:, i, half(h)]
            )
            return tv_ps

        def theta_piece(step):
            if step in piece_steps:
                regroup, op, g, hp = later_pieces[piece_steps.index(step)]
                pieces[step] = regroup(g, hp)
            if step - 1 in pieces:
                regroup, op, g, hp = later_pieces[piece_steps.index(step - 1)]
                quantise(view(op, g, half(hp)), pieces[step - 1][:])

        pieces = {}
        for i in range(BLOCKS):
            if i % 2 == 0 and i + 2 < BLOCKS:
                turned = [turn(src_sb[:, i + 2 + n, :]) for n in range(2)]
                for n in range(2):
                    quantise_src(group_src(turned[n]), i + 2 + n)
            train_view(i, 0, nc.scalar.copy)
            tv_turned = sums.tile([P, PACK, P], F32, tag="sum")
            for t in range(PACK):
                u, e = divmod(t, 2)
                mx_group(
                    nc, tv_turned[:, t, :],
                    [
                        (view(theta_k_q, c, block(2 * e + u)), src_rows(i, c))
                        for c in range(PASSES)
                    ],
                )
            theta_piece(i)
            if i % 2 == 0:
                if i > 0:
                    quantise(view(train_view_q, 0, pair(i // 2 - 1)), tv_grouped[:])
                tv_grouped = stage.tile([P, 2 * P * PACK], BF16, align_bytes=64, tag="tv_grouped")
            nc.scalar.copy(
                out=tv_grouped[:].rearrange("p (n r t) -> p n r t", n=2, t=PACK)[:, i % 2],
                in_=tv_turned[:].rearrange("p t r -> p r t"),
            )
        quantise(view(train_view_q, 0, pair(BLOCKS // 2 - 1)), tv_grouped[:])

        def turn_run(j, w_pair):
            tv = None if j is None else turn_train_view(j)
            w = None if w_pair is None else [turn(w_sb[:, 2 * w_pair + n, :]) for n in range(2)]
            return (
                None if tv is None else group_train_view(tv),
                None if w is None else group_w(w),
            )

        def quantise_run(j, w_pair, tv, w):
            if tv is not None:
                quantise(view(train_view_q, 1, pair(j)), tv[:])
            if w is not None:
                quantise_w(w, w_pair)

        runs = {0: (None, 0), 2: (None, 1), 4: (0, None), 6: (1, None)}
        for i in range(BLOCKS):
            if i in runs:
                run = turn_run(*runs[i])
            copy = nc.vector.tensor_copy if i % 4 == 1 else nc.scalar.copy
            round_train_view(train_view(i, 1, copy), i, copy)
            if i - 1 in runs:
                quantise_run(*runs[i - 1], *run)
            add_bias(i, 0, nc.vector)

        runs = {0: (2, 2), 2: (3, 3)}
        for h in range(HALVES):
            for i in range(BLOCKS):
                if h == 0 and i in runs:
                    run = turn_run(*runs[i])
                if h == 0:
                    theta_piece(BLOCKS + i)
                parts = 2 if (i, h) == (BLOCKS - 1, HALVES - 1) else 1
                width = N_TILE // parts
                for part in range(parts):
                    columns = slice(h * N_TILE + part * width, h * N_TILE + (part + 1) * width)
                    err_ps = sums.tile([P, width], F32, tag="sum")
                    mx_group(
                        nc, err_ps[:],
                        [(src_rows(i, c), view(minus_theta_v_q, c, columns)) for c in range(PASSES)]
                        + [(view(train_view_q, g, block(i)), view(w_q, g, columns)) for g in range(PASSES)],
                    )
                    err_sb = results.tile([P, width], F32, name="err_sb")
                    nc.vector.tensor_tensor(
                        out=err_sb[:],
                        in0=err_ps[:],
                        in1=biased[i, h][:, part * width : (part + 1) * width],
                        op=ADD,
                    )
                    nc.sync.dma_start(out=err_blocks[:, i, columns], in_=err_sb[:])
                if h == 0 and i - 1 in runs:
                    quantise_run(*runs[i - 1], *run)
                if h == 0 and i >= BLOCKS - 3:
                    add_bias(i - BLOCKS + 3, 1, nc.vector)
                if h == 1 and i + 3 < BLOCKS:
                    add_bias(i + 3, 1, nc.gpsimd)
